import numpy as np
import ml_dtypes

BF16 = ml_dtypes.bfloat16


def bf(x):
    return np.asarray(x, np.float32).astype(BF16)


def f32(x):
    return np.asarray(x, np.float32)


def f64(x):
    return np.asarray(x).astype(np.float64)


def striped(idx):
    return np.tile(idx.reshape(-1, 16).T, (8, 1))


C, S, K, M, N = 128, 2048, 4, 128, 8192


def elu(v):
    return np.maximum(v, 0.0) + np.exp(np.minimum(v, 0.0)) - 1.0


def setup_inputs():
    return {"x": bf(np.random.standard_normal((C, S))), "w": bf(np.random.standard_normal((C, M)) / np.sqrt(2.0 * C)), "w_self": bf(np.random.standard_normal((C, M)) / np.sqrt(2.0 * C)), "b": f32(0.1 * np.random.standard_normal((M, 1))), "offs": striped(np.concatenate([np.random.permutation(S) for _ in range(-(-(N) // S))])[:N])}


def reference(x, w, w_self, b, offs):
    idx = offs[:16].T.reshape(-1)
    xs = f64(x)
    ctr = f64(w_self).T @ xs - f64(w).T @ xs + f64(b)
    e = (f64(w).T @ xs[:, idx]).reshape(M, K, S) + ctr[:, None, :]
    return elu(e).max(axis=1)

@@ -1,0 +1,78 @@
+import concourse.mybir as mybir
+
+BF16, F32, U16 = mybir.dt.bfloat16, mybir.dt.float32, mybir.dt.uint16
+ALU = mybir.AluOpType
+FUNC = mybir.ActivationFunctionType
+
+C = 128
+M = 128
+S = 2048
+K = 4
+N = K * S
+PIECE = 512
+BLOCKS = S // PIECE
+
+FLOPS = 2 * C * M * N + 2 * (2 * C * M * S)
+
+
+def tile_edgeconv_kernel(tc, x, w, w_self, b, offs, out):
+    nc = tc.nc
+    with (
+        tc.tile_pool(name="held", bufs=1) as held,
+        tc.tile_pool(name="work", bufs=3) as work,
+        tc.psum_pool(name="banks", bufs=8) as banks,
+    ):
+        offsets = held.tile([128, N // 16], U16, name="offsets")
+        table = held.tile([C, S], BF16, name="table")
+        w_self_sb = held.tile([C, M], BF16, name="w_self_sb")
+        w_sb = held.tile([C, M], BF16, name="w_sb")
+        bias = held.tile([M, 1], F32, name="bias")
+        nc.scalar.dma_start(w_self_sb[:], w_self)
+        nc.scalar.dma_start(w_sb[:], w)
+        for n in range(BLOCKS):
+            cols = slice(n * PIECE, (n + 1) * PIECE)
+            queue = nc.sync if n % 2 == 0 else nc.scalar
+            queue.dma_start(table[:, cols], x[:, cols])
+        nc.sync.dma_start(offsets[:], offs)
+        nc.scalar.dma_start(bias[:], b)
+
+        neg_w = held.tile([C, M], BF16, name="neg_w")
+        nc.vector.tensor_scalar_mul(neg_w[:], w_sb[:], -1.0)
+
+        centre = held.tile([M, S], F32, name="centre")
+        for n in range(BLOCKS):
+            cols = slice(n * PIECE, (n + 1) * PIECE)
+            centre_bank = banks.tile([M, PIECE], F32, name="centre_bank", tag="bank")
+            nc.tensor.matmul(centre_bank[:], w_self_sb[:], table[:, cols], start=True, stop=False)
+            nc.tensor.matmul(centre_bank[:], neg_w[:], table[:, cols], start=False, stop=True)
+            nc.scalar.activation(centre[:, cols], centre_bank[:], FUNC.Identity, bias=bias[:, 0:1])
+
+        for n in range(BLOCKS):
+            cols = slice(n * PIECE, (n + 1) * PIECE)
+
+            products = []
+            for k in range(K):
+                first = (k * S + n * PIECE) // 16
+                product = banks.tile([M, PIECE], F32, name="product", tag="bank")
+                nc.tensor.matmul(
+                    product[:],
+                    w_sb[:],
+                    table[:].indirect(offsets[:, first : first + PIECE // 16]),
+                    start=True,
+                    stop=True,
+                )
+                products.append(product)
+
+            best = work.tile([M, PIECE], F32, name="best")
+            nc.scalar.copy(best[:], products[0][:])
+            for k in range(1, K):
+                nc.vector.tensor_max(best[:], best[:], products[k][:])
+
+            v = work.tile([M, PIECE], F32, name="v")
+            nc.vector.tensor_add(v[:], best[:], centre[:, cols])
+            below = work.tile([M, PIECE], F32, name="below")
+            nc.scalar.activation(below[:], v[:], FUNC.Relu, scale=-1.0)
+            nc.scalar.activation(below[:], below[:], FUNC.Exp, scale=-1.0)
+            result = work.tile([M, PIECE], F32, name="result")
+            nc.vector.scalar_tensor_tensor(result[:], below[:], -1.0, v[:], op0=ALU.add, op1=ALU.max)
+            nc.sync.dma_start(out[:, cols], result[:])

@@ -47,32 +47,39 @@ def tile_edgeconv_kernel(tc, x, w, w_self, b, offs, out):
             nc.tensor.matmul(centre_bank[:], neg_w[:], table[:, cols], start=False, stop=True)
             nc.scalar.activation(centre[:, cols], centre_bank[:], FUNC.Identity, bias=bias[:, 0:1])
 
-        for n in range(BLOCKS):
-            cols = slice(n * PIECE, (n + 1) * PIECE)
+        values = []
+        for n in range(BLOCKS + 1):
+            if n < BLOCKS:
+                cols = slice(n * PIECE, (n + 1) * PIECE)
 
-            products = []
-            for k in range(K):
-                first = (k * S + n * PIECE) // 16
-                product = banks.tile([M, PIECE], F32, name="product", tag="bank")
-                nc.tensor.matmul(
-                    product[:],
-                    w_sb[:],
-                    table[:].indirect(offsets[:, first : first + PIECE // 16]),
-                    start=True,
-                    stop=True,
-                )
-                products.append(product)
+                products = []
+                for k in range(K):
+                    first = (k * S + n * PIECE) // 16
+                    product = banks.tile([M, PIECE], F32, name="product", tag="bank")
+                    nc.tensor.matmul(
+                        product[:],
+                        w_sb[:],
+                        table[:].indirect(offsets[:, first : first + PIECE // 16]),
+                        start=True,
+                        stop=True,
+                    )
+                    products.append(product)
 
-            best = work.tile([M, PIECE], F32, name="best")
-            nc.scalar.copy(best[:], products[0][:])
-            for k in range(1, K):
-                nc.vector.tensor_max(best[:], best[:], products[k][:])
+                best = work.tile([M, PIECE], F32, name="best")
+                nc.scalar.copy(best[:], products[0][:])
+                for k in range(1, K):
+                    nc.vector.tensor_max(best[:], best[:], products[k][:])
 
-            v = work.tile([M, PIECE], F32, name="v")
-            nc.vector.tensor_add(v[:], best[:], centre[:, cols])
-            below = work.tile([M, PIECE], F32, name="below")
-            nc.scalar.activation(below[:], v[:], FUNC.Relu, scale=-1.0)
-            nc.scalar.activation(below[:], below[:], FUNC.Exp, scale=-1.0)
-            result = work.tile([M, PIECE], F32, name="result")
-            nc.vector.scalar_tensor_tensor(result[:], below[:], -1.0, v[:], op0=ALU.add, op1=ALU.max)
-            nc.sync.dma_start(out[:, cols], result[:])
+                v = work.tile([M, PIECE], F32, name="v")
+                nc.vector.tensor_add(v[:], best[:], centre[:, cols])
+                values.append(v)
+
+            if n >= 1:
+                cols = slice((n - 1) * PIECE, n * PIECE)
+                v = values[n - 1]
+                below = work.tile([M, PIECE], F32, name="below")
+                nc.scalar.activation(below[:], v[:], FUNC.Relu, scale=-1.0)
+                nc.scalar.activation(below[:], below[:], FUNC.Exp, scale=-1.0)
+                result = work.tile([M, PIECE], F32, name="result")
+                nc.vector.scalar_tensor_tensor(result[:], below[:], -1.0, v[:], op0=ALU.add, op1=ALU.max)
+                nc.sync.dma_start(out[:, cols], result[:])

@@ -11,6 +11,7 @@ K = 4
 N = K * S
 PIECE = 512
 BLOCKS = S // PIECE
+HALVES = (slice(0, PIECE // 2), slice(PIECE // 2, PIECE))
 
 FLOPS = 2 * C * M * N + 2 * (2 * C * M * S)
 
@@ -47,39 +48,43 @@ def tile_edgeconv_kernel(tc, x, w, w_self, b, offs, out):
             nc.tensor.matmul(centre_bank[:], neg_w[:], table[:, cols], start=False, stop=True)
             nc.scalar.activation(centre[:, cols], centre_bank[:], FUNC.Identity, bias=bias[:, 0:1])
 
-        values = []
-        for n in range(BLOCKS + 1):
-            if n < BLOCKS:
-                cols = slice(n * PIECE, (n + 1) * PIECE)
+        for n in range(BLOCKS):
+            cols = slice(n * PIECE, (n + 1) * PIECE)
 
-                products = []
-                for k in range(K):
-                    first = (k * S + n * PIECE) // 16
-                    product = banks.tile([M, PIECE], F32, name="product", tag="bank")
-                    nc.tensor.matmul(
-                        product[:],
-                        w_sb[:],
-                        table[:].indirect(offsets[:, first : first + PIECE // 16]),
-                        start=True,
-                        stop=True,
-                    )
-                    products.append(product)
+            products = []
+            for k in range(K):
+                first = (k * S + n * PIECE) // 16
+                product = banks.tile([M, PIECE], F32, name="product", tag="bank")
+                nc.tensor.matmul(
+                    product[:],
+                    w_sb[:],
+                    table[:].indirect(offsets[:, first : first + PIECE // 16]),
+                    start=True,
+                    stop=True,
+                )
+                products.append(product)
 
-                best = work.tile([M, PIECE], F32, name="best")
-                nc.scalar.copy(best[:], products[0][:])
-                for k in range(1, K):
-                    nc.vector.tensor_max(best[:], best[:], products[k][:])
+            best = work.tile([M, PIECE], F32, name="best")
+            nc.scalar.copy(best[:], products[0][:])
+            for k in range(1, K):
+                for half in HALVES:
+                    nc.vector.tensor_max(best[:, half], best[:, half], products[k][:, half])
 
-                v = work.tile([M, PIECE], F32, name="v")
-                nc.vector.tensor_add(v[:], best[:], centre[:, cols])
-                values.append(v)
-
-            if n >= 1:
-                cols = slice((n - 1) * PIECE, n * PIECE)
-                v = values[n - 1]
-                below = work.tile([M, PIECE], F32, name="below")
-                nc.scalar.activation(below[:], v[:], FUNC.Relu, scale=-1.0)
-                nc.scalar.activation(below[:], below[:], FUNC.Exp, scale=-1.0)
-                result = work.tile([M, PIECE], F32, name="result")
-                nc.vector.scalar_tensor_tensor(result[:], below[:], -1.0, v[:], op0=ALU.add, op1=ALU.max)
-                nc.sync.dma_start(out[:, cols], result[:])
+            v = work.tile([M, PIECE], F32, name="v")
+            block_centre = centre[:, cols]
+            if n < BLOCKS - 1:
+                nc.gpsimd.tensor_add(v[:], best[:], block_centre)
+            else:
+                for half in HALVES:
+                    nc.vector.tensor_add(v[:, half], best[:, half], block_centre[:, half])
+            grown = work.tile([M, PIECE], F32, name="grown")
+            kept = work.tile([M, PIECE], F32, name="kept")
+            for half in HALVES:
+                nc.scalar.activation(grown[:, half], v[:, half], FUNC.Exp)
+                nc.scalar.activation(kept[:, half], v[:, half], FUNC.Relu)
+            result = work.tile([M, PIECE], F32, name="result")
+            for half in HALVES:
+                nc.vector.scalar_tensor_tensor(
+                    result[:, half], grown[:, half], -1.0, kept[:, half], op0=ALU.add, op1=ALU.min
+                )
+            nc.sync.dma_start(out[:, cols], result[:])

@@ -11,7 +11,9 @@ K = 4
 N = K * S
 PIECE = 512
 BLOCKS = S // PIECE
-HALVES = (slice(0, PIECE // 2), slice(PIECE // 2, PIECE))
+PARTS = [slice(i * PIECE // 2, (i + 1) * PIECE // 2) for i in range(2)]
+WARM_UP = 3
+SKEW = 2
 
 FLOPS = 2 * C * M * N + 2 * (2 * C * M * S)
 
@@ -20,7 +22,7 @@ def tile_edgeconv_kernel(tc, x, w, w_self, b, offs, out):
     nc = tc.nc
     with (
         tc.tile_pool(name="held", bufs=1) as held,
-        tc.tile_pool(name="work", bufs=3) as work,
+        tc.tile_pool(name="work", bufs=4) as work,
         tc.psum_pool(name="banks", bufs=8) as banks,
     ):
         offsets = held.tile([128, N // 16], U16, name="offsets")
@@ -37,6 +39,12 @@ def tile_edgeconv_kernel(tc, x, w, w_self, b, offs, out):
         nc.sync.dma_start(offsets[:], offs)
         nc.scalar.dma_start(bias[:], b)
 
+        zeros = held.tile([C, PIECE], BF16, name="zeros")
+        nc.vector.memset(zeros[:], 0.0)
+        unused = banks.tile([M, PIECE], F32, name="unused", tag="bank")
+        for i in range(WARM_UP):
+            nc.tensor.matmul(unused[:], zeros[:, 0:M], zeros[:], start=True, stop=True)
+
         neg_w = held.tile([C, M], BF16, name="neg_w")
         nc.vector.tensor_scalar_mul(neg_w[:], w_sb[:], -1.0)
 
@@ -46,45 +54,54 @@ def tile_edgeconv_kernel(tc, x, w, w_self, b, offs, out):
             centre_bank = banks.tile([M, PIECE], F32, name="centre_bank", tag="bank")
             nc.tensor.matmul(centre_bank[:], w_self_sb[:], table[:, cols], start=True, stop=False)
             nc.tensor.matmul(centre_bank[:], neg_w[:], table[:, cols], start=False, stop=True)
-            nc.scalar.activation(centre[:, cols], centre_bank[:], FUNC.Identity, bias=bias[:, 0:1])
+            nc.scalar.copy(centre[:, cols], centre_bank[:])
 
-        for n in range(BLOCKS):
-            cols = slice(n * PIECE, (n + 1) * PIECE)
+        values = []
+        for step in range(BLOCKS + SKEW):
+            if step < BLOCKS:
+                n = step
+                cols = slice(n * PIECE, (n + 1) * PIECE)
+                products = []
+                for k in range(K):
+                    first = (k * S + n * PIECE) // 16
+                    product = banks.tile([M, PIECE], F32, name="product", tag="bank")
+                    nc.tensor.matmul(
+                        product[:],
+                        w_sb[:],
+                        table[:].indirect(offsets[:, first : first + PIECE // 16]),
+                        start=True,
+                        stop=True,
+                    )
+                    products.append(product)
 
-            products = []
-            for k in range(K):
-                first = (k * S + n * PIECE) // 16
-                product = banks.tile([M, PIECE], F32, name="product", tag="bank")
-                nc.tensor.matmul(
-                    product[:],
-                    w_sb[:],
-                    table[:].indirect(offsets[:, first : first + PIECE // 16]),
-                    start=True,
-                    stop=True,
-                )
-                products.append(product)
+                best = work.tile([M, PIECE], F32, name="best")
+                for part in PARTS:
+                    nc.scalar.copy(best[:, part], products[0][:, part])
+                for k in range(1, K):
+                    for part in PARTS:
+                        nc.vector.tensor_max(best[:, part], best[:, part], products[k][:, part])
 
-            best = work.tile([M, PIECE], F32, name="best")
-            nc.scalar.copy(best[:], products[0][:])
-            for k in range(1, K):
-                for half in HALVES:
-                    nc.vector.tensor_max(best[:, half], best[:, half], products[k][:, half])
+                v = work.tile([M, PIECE], F32, name="v")
+                block_centre = centre[:, cols]
+                if n < BLOCKS - 1:
+                    nc.gpsimd.tensor_add(v[:], best[:], block_centre)
+                else:
+                    for part in PARTS:
+                        nc.vector.tensor_add(v[:, part], best[:, part], block_centre[:, part])
+                values.append(v)
 
-            v = work.tile([M, PIECE], F32, name="v")
-            block_centre = centre[:, cols]
-            if n < BLOCKS - 1:
-                nc.gpsimd.tensor_add(v[:], best[:], block_centre)
-            else:
-                for half in HALVES:
-                    nc.vector.tensor_add(v[:, half], best[:, half], block_centre[:, half])
-            grown = work.tile([M, PIECE], F32, name="grown")
-            kept = work.tile([M, PIECE], F32, name="kept")
-            for half in HALVES:
-                nc.scalar.activation(grown[:, half], v[:, half], FUNC.Exp)
-                nc.scalar.activation(kept[:, half], v[:, half], FUNC.Relu)
-            result = work.tile([M, PIECE], F32, name="result")
-            for half in HALVES:
-                nc.vector.scalar_tensor_tensor(
-                    result[:, half], grown[:, half], -1.0, kept[:, half], op0=ALU.add, op1=ALU.min
-                )
-            nc.sync.dma_start(out[:, cols], result[:])
+            if step >= SKEW:
+                n = step - SKEW
+                cols = slice(n * PIECE, (n + 1) * PIECE)
+                v = values[n]
+                grown = work.tile([M, PIECE], F32, name="grown")
+                kept = work.tile([M, PIECE], F32, name="kept")
+                for part in PARTS:
+                    nc.scalar.activation(grown[:, part], v[:, part], FUNC.Exp, bias=bias[:, 0:1])
+                    nc.scalar.activation(kept[:, part], v[:, part], FUNC.Relu, bias=bias[:, 0:1])
+                result = work.tile([M, PIECE], F32, name="result")
+                for part in PARTS:
+                    nc.vector.scalar_tensor_tensor(
+                        result[:, part], grown[:, part], -1.0, kept[:, part], op0=ALU.add, op1=ALU.min
+                    )
+                nc.sync.dma_start(out[:, cols], result[:])

@@ -11,7 +11,7 @@ K = 4
 N = K * S
 PIECE = 512
 BLOCKS = S // PIECE
-PARTS = [slice(i * PIECE // 2, (i + 1) * PIECE // 2) for i in range(2)]
+HALVES = (slice(0, PIECE // 2), slice(PIECE // 2, PIECE))
 WARM_UP = 3
 SKEW = 2
 
@@ -22,7 +22,7 @@ def tile_edgeconv_kernel(tc, x, w, w_self, b, offs, out):
     nc = tc.nc
     with (
         tc.tile_pool(name="held", bufs=1) as held,
-        tc.tile_pool(name="work", bufs=4) as work,
+        tc.tile_pool(name="work", bufs=BLOCKS) as work,
         tc.psum_pool(name="banks", bufs=8) as banks,
     ):
         offsets = held.tile([128, N // 16], U16, name="offsets")
@@ -56,11 +56,12 @@ def tile_edgeconv_kernel(tc, x, w, w_self, b, offs, out):
             nc.tensor.matmul(centre_bank[:], neg_w[:], table[:, cols], start=False, stop=True)
             nc.scalar.copy(centre[:, cols], centre_bank[:])
 
-        values = []
+        sums = []
         for step in range(BLOCKS + SKEW):
             if step < BLOCKS:
                 n = step
                 cols = slice(n * PIECE, (n + 1) * PIECE)
+
                 products = []
                 for k in range(K):
                     first = (k * S + n * PIECE) // 16
@@ -74,34 +75,40 @@ def tile_edgeconv_kernel(tc, x, w, w_self, b, offs, out):
                     )
                     products.append(product)
 
-                best = work.tile([M, PIECE], F32, name="best")
-                for part in PARTS:
-                    nc.scalar.copy(best[:, part], products[0][:, part])
+                best = work.tile([M, PIECE], F32, name="best", bufs=BLOCKS - 1)
+                for half in HALVES:
+                    nc.scalar.copy(best[:, half], products[0][:, half])
                 for k in range(1, K):
-                    for part in PARTS:
-                        nc.vector.tensor_max(best[:, part], best[:, part], products[k][:, part])
+                    for half in HALVES:
+                        nc.vector.tensor_max(best[:, half], best[:, half], products[k][:, half])
 
-                v = work.tile([M, PIECE], F32, name="v")
+                total = work.tile([M, PIECE], F32, name="total")
                 block_centre = centre[:, cols]
                 if n < BLOCKS - 1:
-                    nc.gpsimd.tensor_add(v[:], best[:], block_centre)
+                    nc.gpsimd.tensor_add(total[:], best[:], block_centre)
                 else:
-                    for part in PARTS:
-                        nc.vector.tensor_add(v[:, part], best[:, part], block_centre[:, part])
-                values.append(v)
+                    for half in HALVES:
+                        nc.vector.tensor_add(total[:, half], best[:, half], block_centre[:, half])
+                sums.append(total)
 
             if step >= SKEW:
                 n = step - SKEW
                 cols = slice(n * PIECE, (n + 1) * PIECE)
-                v = values[n]
+                total = sums[n]
+
                 grown = work.tile([M, PIECE], F32, name="grown")
                 kept = work.tile([M, PIECE], F32, name="kept")
-                for part in PARTS:
-                    nc.scalar.activation(grown[:, part], v[:, part], FUNC.Exp, bias=bias[:, 0:1])
-                    nc.scalar.activation(kept[:, part], v[:, part], FUNC.Relu, bias=bias[:, 0:1])
                 result = work.tile([M, PIECE], F32, name="result")
-                for part in PARTS:
+                for half in HALVES:
+                    nc.scalar.activation(grown[:, half], total[:, half], FUNC.Exp, bias=bias[:, 0:1])
+                    if n < BLOCKS - 1:
+                        nc.scalar.activation(kept[:, half], total[:, half], FUNC.Relu, bias=bias[:, 0:1])
+                    else:
+                        nc.vector.tensor_scalar(
+                            kept[:, half], total[:, half], bias[:, 0:1], 0.0, op0=ALU.add, op1=ALU.max
+                        )
+                for half in HALVES:
                     nc.vector.scalar_tensor_tensor(
-                        result[:, part], grown[:, part], -1.0, kept[:, part], op0=ALU.add, op1=ALU.min
+                        result[:, half], grown[:, half], -1.0, kept[:, half], op0=ALU.add, op1=ALU.min
                     )
                 nc.sync.dma_start(out[:, cols], result[:])

@@ -101,12 +101,7 @@ def tile_edgeconv_kernel(tc, x, w, w_self, b, offs, out):
                 result = work.tile([M, PIECE], F32, name="result")
                 for half in HALVES:
                     nc.scalar.activation(grown[:, half], total[:, half], FUNC.Exp, bias=bias[:, 0:1])
-                    if n < BLOCKS - 1:
-                        nc.scalar.activation(kept[:, half], total[:, half], FUNC.Relu, bias=bias[:, 0:1])
-                    else:
-                        nc.vector.tensor_scalar(
-                            kept[:, half], total[:, half], bias[:, 0:1], 0.0, op0=ALU.add, op1=ALU.max
-                        )
+                    nc.scalar.activation(kept[:, half], total[:, half], FUNC.Relu, bias=bias[:, 0:1])
                 for half in HALVES:
                     nc.vector.scalar_tensor_tensor(
                         result[:, half], grown[:, half], -1.0, kept[:, half], op0=ALU.add, op1=ALU.min

@@ -14,6 +14,7 @@ BLOCKS = S // PIECE
 HALVES = (slice(0, PIECE // 2), slice(PIECE // 2, PIECE))
 WARM_UP = 3
 SKEW = 2
+EARLY = BLOCKS - 1
 
 FLOPS = 2 * C * M * N + 2 * (2 * C * M * S)
 
@@ -32,11 +33,12 @@ def tile_edgeconv_kernel(tc, x, w, w_self, b, offs, out):
         bias = held.tile([M, 1], F32, name="bias")
         nc.scalar.dma_start(w_self_sb[:], w_self)
         nc.scalar.dma_start(w_sb[:], w)
-        for n in range(BLOCKS):
+        nc.sync.dma_start(table[:, 0:PIECE], x[:, 0:PIECE])
+        nc.sync.dma_start(offsets[:], offs)
+        for n in range(1, BLOCKS):
             cols = slice(n * PIECE, (n + 1) * PIECE)
             queue = nc.sync if n % 2 == 0 else nc.scalar
             queue.dma_start(table[:, cols], x[:, cols])
-        nc.sync.dma_start(offsets[:], offs)
         nc.scalar.dma_start(bias[:], b)
 
         zeros = held.tile([C, PIECE], BF16, name="zeros")
@@ -48,13 +50,17 @@ def tile_edgeconv_kernel(tc, x, w, w_self, b, offs, out):
         neg_w = held.tile([C, M], BF16, name="neg_w")
         nc.vector.tensor_scalar_mul(neg_w[:], w_sb[:], -1.0)
 
-        centre = held.tile([M, S], F32, name="centre")
-        for n in range(BLOCKS):
+        def centre_term(n):
             cols = slice(n * PIECE, (n + 1) * PIECE)
             centre_bank = banks.tile([M, PIECE], F32, name="centre_bank", tag="bank")
             nc.tensor.matmul(centre_bank[:], w_self_sb[:], table[:, cols], start=True, stop=False)
             nc.tensor.matmul(centre_bank[:], neg_w[:], table[:, cols], start=False, stop=True)
-            nc.scalar.copy(centre[:, cols], centre_bank[:])
+            return centre_bank
+
+        centre = held.tile([M, EARLY * PIECE], F32, name="centre")
+        for n in range(EARLY):
+            cols = slice(n * PIECE, (n + 1) * PIECE)
+            nc.scalar.copy(centre[:, cols], centre_term(n)[:])
 
         sums = []
         for step in range(BLOCKS + SKEW):
@@ -83,12 +89,12 @@ def tile_edgeconv_kernel(tc, x, w, w_self, b, offs, out):
                         nc.vector.tensor_max(best[:, half], best[:, half], products[k][:, half])
 
                 total = work.tile([M, PIECE], F32, name="total")
-                block_centre = centre[:, cols]
-                if n < BLOCKS - 1:
-                    nc.gpsimd.tensor_add(total[:], best[:], block_centre)
+                if n < EARLY:
+                    nc.gpsimd.tensor_add(total[:], best[:], centre[:, cols])
                 else:
+                    late_centre = centre_term(n)
                     for half in HALVES:
-                        nc.vector.tensor_add(total[:, half], best[:, half], block_centre[:, half])
+                        nc.vector.tensor_add(total[:, half], best[:, half], late_centre[:, half])
                 sums.append(total)
 
             if step >= SKEW:

@@ -14,7 +14,7 @@ BLOCKS = S // PIECE
 HALVES = (slice(0, PIECE // 2), slice(PIECE // 2, PIECE))
 WARM_UP = 3
 SKEW = 2
-EARLY = BLOCKS - 1
+GPSIMD_BLOCKS = BLOCKS // 2
 
 FLOPS = 2 * C * M * N + 2 * (2 * C * M * S)
 
@@ -57,54 +57,53 @@ def tile_edgeconv_kernel(tc, x, w, w_self, b, offs, out):
             nc.tensor.matmul(centre_bank[:], neg_w[:], table[:, cols], start=False, stop=True)
             return centre_bank
 
-        centre = held.tile([M, EARLY * PIECE], F32, name="centre")
-        for n in range(EARLY):
-            cols = slice(n * PIECE, (n + 1) * PIECE)
-            nc.scalar.copy(centre[:, cols], centre_term(n)[:])
-
-        sums = []
-        for step in range(BLOCKS + SKEW):
-            if step < BLOCKS:
-                n = step
-                cols = slice(n * PIECE, (n + 1) * PIECE)
-
-                products = []
-                for k in range(K):
-                    first = (k * S + n * PIECE) // 16
-                    product = banks.tile([M, PIECE], F32, name="product", tag="bank")
-                    nc.tensor.matmul(
-                        product[:],
-                        w_sb[:],
-                        table[:].indirect(offsets[:, first : first + PIECE // 16]),
-                        start=True,
-                        stop=True,
-                    )
-                    products.append(product)
-
-                best = work.tile([M, PIECE], F32, name="best", bufs=BLOCKS - 1)
+        def maximum(n):
+            products = []
+            for k in range(K):
+                first = (k * S + n * PIECE) // 16
+                product = banks.tile([M, PIECE], F32, name="product", tag="bank")
+                nc.tensor.matmul(
+                    product[:],
+                    w_sb[:],
+                    table[:].indirect(offsets[:, first : first + PIECE // 16]),
+                    start=True,
+                    stop=True,
+                )
+                products.append(product)
+            best = work.tile([M, PIECE], F32, name="best")
+            for half in HALVES:
+                nc.scalar.copy(best[:, half], products[0][:, half])
+            for k in range(1, K):
                 for half in HALVES:
-                    nc.scalar.copy(best[:, half], products[0][:, half])
-                for k in range(1, K):
-                    for half in HALVES:
-                        nc.vector.tensor_max(best[:, half], best[:, half], products[k][:, half])
+                    nc.vector.tensor_max(best[:, half], best[:, half], products[k][:, half])
+            return best
 
-                total = work.tile([M, PIECE], F32, name="total")
-                if n < EARLY:
-                    nc.gpsimd.tensor_add(total[:], best[:], centre[:, cols])
-                else:
-                    late_centre = centre_term(n)
-                    for half in HALVES:
-                        nc.vector.tensor_add(total[:, half], best[:, half], late_centre[:, half])
-                sums.append(total)
+        centre = held.tile([M, GPSIMD_BLOCKS * PIECE], F32, name="centre")
+        for n in range(GPSIMD_BLOCKS):
+            nc.scalar.copy(centre[:, n * PIECE : (n + 1) * PIECE], centre_term(n)[:])
+        centre_banks = {n: centre_term(n) for n in range(GPSIMD_BLOCKS, BLOCKS - 1)}
 
-            if step >= SKEW:
-                n = step - SKEW
-                cols = slice(n * PIECE, (n + 1) * PIECE)
-                total = sums[n]
+        def add_centre(n, best):
+            total = work.tile([M, PIECE], F32, name="total")
+            if n < GPSIMD_BLOCKS:
+                nc.gpsimd.tensor_add(total[:], best[:], centre[:, n * PIECE : (n + 1) * PIECE])
+            else:
+                centre_bank = centre_banks[n] if n in centre_banks else centre_term(n)
+                for half in HALVES:
+                    nc.vector.tensor_add(total[:, half], best[:, half], centre_bank[:, half])
+            return total
 
-                grown = work.tile([M, PIECE], F32, name="grown")
-                kept = work.tile([M, PIECE], F32, name="kept")
-                result = work.tile([M, PIECE], F32, name="result")
+        def elu(n, total):
+            grown = work.tile([M, PIECE], F32, name="grown")
+            kept = work.tile([M, PIECE], F32, name="kept")
+            result = work.tile([M, PIECE], F32, name="result")
+            if n < GPSIMD_BLOCKS:
+                lost = work.tile([M, PIECE], F32, name="lost", bufs=GPSIMD_BLOCKS)
+                nc.scalar.activation(grown[:], total[:], FUNC.Exp, bias=bias[:, 0:1])
+                nc.scalar.activation(kept[:], total[:], FUNC.Relu, bias=bias[:, 0:1])
+                nc.scalar.activation(lost[:], grown[:], FUNC.Relu, bias=1.0, scale=-1.0)
+                nc.gpsimd.tensor_sub(result[:], kept[:], lost[:])
+            else:
                 for half in HALVES:
                     nc.scalar.activation(grown[:, half], total[:, half], FUNC.Exp, bias=bias[:, 0:1])
                     nc.scalar.activation(kept[:, half], total[:, half], FUNC.Relu, bias=bias[:, 0:1])
@@ -112,4 +111,11 @@ def tile_edgeconv_kernel(tc, x, w, w_self, b, offs, out):
                     nc.vector.scalar_tensor_tensor(
                         result[:, half], grown[:, half], -1.0, kept[:, half], op0=ALU.add, op1=ALU.min
                     )
-                nc.sync.dma_start(out[:, cols], result[:])
+            nc.sync.dma_start(out[:, n * PIECE : (n + 1) * PIECE], result[:])
+
+        totals = []
+        for step in range(BLOCKS + SKEW):
+            if step < BLOCKS:
+                totals.append(add_centre(step, maximum(step)))
+            if step >= SKEW:
+                elu(step - SKEW, totals[step - SKEW])

@@ -103,6 +103,7 @@ def tile_edgeconv_kernel(tc, x, w, w_self, b, offs, out):
                 nc.scalar.activation(kept[:], total[:], FUNC.Relu, bias=bias[:, 0:1])
                 nc.scalar.activation(lost[:], grown[:], FUNC.Relu, bias=1.0, scale=-1.0)
                 nc.gpsimd.tensor_sub(result[:], kept[:], lost[:])
+                nc.sync.dma_start(out[:, n * PIECE : (n + 1) * PIECE], result[:])
             else:
                 for half in HALVES:
                     nc.scalar.activation(grown[:, half], total[:, half], FUNC.Exp, bias=bias[:, 0:1])
@@ -111,7 +112,7 @@ def tile_edgeconv_kernel(tc, x, w, w_self, b, offs, out):
                     nc.vector.scalar_tensor_tensor(
                         result[:, half], grown[:, half], -1.0, kept[:, half], op0=ALU.add, op1=ALU.min
                     )
-            nc.sync.dma_start(out[:, n * PIECE : (n + 1) * PIECE], result[:])
+                    nc.sync.dma_start(out[:, n * PIECE + half.start : n * PIECE + half.stop], result[:, half])
 
         totals = []
         for step in range(BLOCKS + SKEW):

@@ -11,10 +11,9 @@ K = 4
 N = K * S
 PIECE = 512
 BLOCKS = S // PIECE
-HALVES = (slice(0, PIECE // 2), slice(PIECE // 2, PIECE))
+PARTS = (slice(0, 176), slice(176, 344), slice(344, PIECE))
 WARM_UP = 3
-SKEW = 2
-GPSIMD_BLOCKS = BLOCKS // 2
+JOINED_BY_GPSIMD = BLOCKS // 2
 
 FLOPS = 2 * C * M * N + 2 * (2 * C * M * S)
 
@@ -70,53 +69,56 @@ def tile_edgeconv_kernel(tc, x, w, w_self, b, offs, out):
                     stop=True,
                 )
                 products.append(product)
-            best = work.tile([M, PIECE], F32, name="best")
-            for half in HALVES:
-                nc.scalar.copy(best[:, half], products[0][:, half])
+            best = work.tile([M, PIECE], F32, name="best", bufs=2)
+            for part in PARTS:
+                nc.scalar.copy(best[:, part], products[0][:, part])
             for k in range(1, K):
-                for half in HALVES:
-                    nc.vector.tensor_max(best[:, half], best[:, half], products[k][:, half])
+                for part in PARTS:
+                    nc.vector.tensor_max(best[:, part], best[:, part], products[k][:, part])
             return best
 
-        centre = held.tile([M, GPSIMD_BLOCKS * PIECE], F32, name="centre")
-        for n in range(GPSIMD_BLOCKS):
-            nc.scalar.copy(centre[:, n * PIECE : (n + 1) * PIECE], centre_term(n)[:])
-        centre_banks = {n: centre_term(n) for n in range(GPSIMD_BLOCKS, BLOCKS - 1)}
+        centre_banks = {n: centre_term(n) for n in range(BLOCKS - 1)}
 
         def add_centre(n, best):
             total = work.tile([M, PIECE], F32, name="total")
-            if n < GPSIMD_BLOCKS:
-                nc.gpsimd.tensor_add(total[:], best[:], centre[:, n * PIECE : (n + 1) * PIECE])
-            else:
-                centre_bank = centre_banks[n] if n in centre_banks else centre_term(n)
-                for half in HALVES:
-                    nc.vector.tensor_add(total[:, half], best[:, half], centre_bank[:, half])
+            centre_bank = centre_banks[n] if n in centre_banks else centre_term(n)
+            for part in PARTS:
+                nc.vector.tensor_add(total[:, part], best[:, part], centre_bank[:, part])
             return total
 
-        def elu(n, total):
+        def exp_and_relu(n, total):
             grown = work.tile([M, PIECE], F32, name="grown")
             kept = work.tile([M, PIECE], F32, name="kept")
-            result = work.tile([M, PIECE], F32, name="result")
-            if n < GPSIMD_BLOCKS:
-                lost = work.tile([M, PIECE], F32, name="lost", bufs=GPSIMD_BLOCKS)
+            if n < BLOCKS - 1:
                 nc.scalar.activation(grown[:], total[:], FUNC.Exp, bias=bias[:, 0:1])
                 nc.scalar.activation(kept[:], total[:], FUNC.Relu, bias=bias[:, 0:1])
+            else:
+                for part in PARTS:
+                    nc.scalar.activation(grown[:, part], total[:, part], FUNC.Exp, bias=bias[:, 0:1])
+                    nc.vector.tensor_scalar(
+                        kept[:, part], total[:, part], bias[:, 0:1], 0.0, op0=ALU.add, op1=ALU.max
+                    )
+            return grown, kept
+
+        def join(n, grown, kept):
+            result = work.tile([M, PIECE], F32, name="result")
+            if n < JOINED_BY_GPSIMD:
+                lost = work.tile([M, PIECE], F32, name="lost", bufs=JOINED_BY_GPSIMD)
                 nc.scalar.activation(lost[:], grown[:], FUNC.Relu, bias=1.0, scale=-1.0)
                 nc.gpsimd.tensor_sub(result[:], kept[:], lost[:])
                 nc.sync.dma_start(out[:, n * PIECE : (n + 1) * PIECE], result[:])
             else:
-                for half in HALVES:
-                    nc.scalar.activation(grown[:, half], total[:, half], FUNC.Exp, bias=bias[:, 0:1])
-                    nc.scalar.activation(kept[:, half], total[:, half], FUNC.Relu, bias=bias[:, 0:1])
-                for half in HALVES:
+                for part in PARTS:
                     nc.vector.scalar_tensor_tensor(
-                        result[:, half], grown[:, half], -1.0, kept[:, half], op0=ALU.add, op1=ALU.min
+                        result[:, part], grown[:, part], -1.0, kept[:, part], op0=ALU.add, op1=ALU.min
                     )
-                    nc.sync.dma_start(out[:, n * PIECE + half.start : n * PIECE + half.stop], result[:, half])
+                    nc.sync.dma_start(out[:, n * PIECE + part.start : n * PIECE + part.stop], result[:, part])
 
-        totals = []
-        for step in range(BLOCKS + SKEW):
+        totals, parts = {}, {}
+        for step in range(BLOCKS + 2):
             if step < BLOCKS:
-                totals.append(add_centre(step, maximum(step)))
-            if step >= SKEW:
-                elu(step - SKEW, totals[step - SKEW])
+                totals[step] = add_centre(step, maximum(step))
+            if 0 <= step - 1 < BLOCKS:
+                parts[step - 1] = exp_and_relu(step - 1, totals[step - 1])
+            if 0 <= step - 2:
+                join(step - 2, *parts[step - 2])

@@ -11,9 +11,11 @@ K = 4
 N = K * S
 PIECE = 512
 BLOCKS = S // PIECE
-PARTS = (slice(0, 176), slice(176, 344), slice(344, PIECE))
+WHOLE = (slice(0, PIECE),)
+HALVES = (slice(0, PIECE // 2), slice(PIECE // 2, PIECE))
 WARM_UP = 3
 JOINED_BY_GPSIMD = BLOCKS // 2
+ADDED_BY_GPSIMD = BLOCKS - 2
 
 FLOPS = 2 * C * M * N + 2 * (2 * C * M * S)
 
@@ -32,13 +34,11 @@ def tile_edgeconv_kernel(tc, x, w, w_self, b, offs, out):
         bias = held.tile([M, 1], F32, name="bias")
         nc.scalar.dma_start(w_self_sb[:], w_self)
         nc.scalar.dma_start(w_sb[:], w)
-        nc.sync.dma_start(table[:, 0:PIECE], x[:, 0:PIECE])
-        nc.sync.dma_start(offsets[:], offs)
-        for n in range(1, BLOCKS):
-            cols = slice(n * PIECE, (n + 1) * PIECE)
-            queue = nc.sync if n % 2 == 0 else nc.scalar
-            queue.dma_start(table[:, cols], x[:, cols])
         nc.scalar.dma_start(bias[:], b)
+        for n in (0, 1):
+            nc.sync.dma_start(table[:, n * PIECE : (n + 1) * PIECE], x[:, n * PIECE : (n + 1) * PIECE])
+        nc.sync.dma_start(offsets[:], offs)
+        nc.sync.dma_start(table[:, 2 * PIECE :], x[:, 2 * PIECE :])
 
         zeros = held.tile([C, PIECE], BF16, name="zeros")
         nc.vector.memset(zeros[:], 0.0)
@@ -70,33 +70,38 @@ def tile_edgeconv_kernel(tc, x, w, w_self, b, offs, out):
                 )
                 products.append(product)
             best = work.tile([M, PIECE], F32, name="best", bufs=2)
-            for part in PARTS:
-                nc.scalar.copy(best[:, part], products[0][:, part])
+            for half in HALVES:
+                nc.scalar.copy(best[:, half], products[0][:, half])
             for k in range(1, K):
-                for part in PARTS:
-                    nc.vector.tensor_max(best[:, part], best[:, part], products[k][:, part])
+                for half in HALVES:
+                    nc.vector.tensor_max(best[:, half], best[:, half], products[k][:, half])
             return best
 
         centre_banks = {n: centre_term(n) for n in range(BLOCKS - 1)}
+        centre = held.tile([M, PIECE], F32, name="centre")
+        nc.scalar.copy(centre[:], centre_banks[ADDED_BY_GPSIMD][:])
 
         def add_centre(n, best):
             total = work.tile([M, PIECE], F32, name="total")
-            centre_bank = centre_banks[n] if n in centre_banks else centre_term(n)
-            for part in PARTS:
-                nc.vector.tensor_add(total[:, part], best[:, part], centre_bank[:, part])
+            if n == ADDED_BY_GPSIMD:
+                for half in HALVES:
+                    nc.gpsimd.tensor_add(total[:, half], best[:, half], centre[:, half])
+            else:
+                centre_bank = centre_banks[n] if n in centre_banks else centre_term(n)
+                for half in HALVES:
+                    nc.vector.tensor_add(total[:, half], best[:, half], centre_bank[:, half])
             return total
 
         def exp_and_relu(n, total):
             grown = work.tile([M, PIECE], F32, name="grown")
             kept = work.tile([M, PIECE], F32, name="kept")
-            if n < BLOCKS - 1:
-                nc.scalar.activation(grown[:], total[:], FUNC.Exp, bias=bias[:, 0:1])
-                nc.scalar.activation(kept[:], total[:], FUNC.Relu, bias=bias[:, 0:1])
-            else:
-                for part in PARTS:
-                    nc.scalar.activation(grown[:, part], total[:, part], FUNC.Exp, bias=bias[:, 0:1])
+            for piece in WHOLE if n < JOINED_BY_GPSIMD else HALVES:
+                nc.scalar.activation(grown[:, piece], total[:, piece], FUNC.Exp, bias=bias[:, 0:1])
+                if n < BLOCKS - 1:
+                    nc.scalar.activation(kept[:, piece], total[:, piece], FUNC.Relu, bias=bias[:, 0:1])
+                else:
                     nc.vector.tensor_scalar(
-                        kept[:, part], total[:, part], bias[:, 0:1], 0.0, op0=ALU.add, op1=ALU.max
+                        kept[:, piece], total[:, piece], bias[:, 0:1], 0.0, op0=ALU.add, op1=ALU.max
                     )
             return grown, kept
 
@@ -108,11 +113,11 @@ def tile_edgeconv_kernel(tc, x, w, w_self, b, offs, out):
                 nc.gpsimd.tensor_sub(result[:], kept[:], lost[:])
                 nc.sync.dma_start(out[:, n * PIECE : (n + 1) * PIECE], result[:])
             else:
-                for part in PARTS:
+                for half in HALVES:
                     nc.vector.scalar_tensor_tensor(
-                        result[:, part], grown[:, part], -1.0, kept[:, part], op0=ALU.add, op1=ALU.min
+                        result[:, half], grown[:, half], -1.0, kept[:, half], op0=ALU.add, op1=ALU.min
                     )
-                    nc.sync.dma_start(out[:, n * PIECE + part.start : n * PIECE + part.stop], result[:, part])
+                    nc.sync.dma_start(out[:, n * PIECE + half.start : n * PIECE + half.stop], result[:, half])
 
         totals, parts = {}, {}
         for step in range(BLOCKS + 2):

@@ -92,38 +92,49 @@ def tile_edgeconv_kernel(tc, x, w, w_self, b, offs, out):
                     nc.vector.tensor_add(total[:, half], best[:, half], centre_bank[:, half])
             return total
 
-        def exp_and_relu(n, total):
-            grown = work.tile([M, PIECE], F32, name="grown")
-            kept = work.tile([M, PIECE], F32, name="kept")
+        def exp(n):
+            grown[n] = work.tile([M, PIECE], F32, name="grown")
             for piece in WHOLE if n < JOINED_BY_GPSIMD else HALVES:
-                nc.scalar.activation(grown[:, piece], total[:, piece], FUNC.Exp, bias=bias[:, 0:1])
+                nc.scalar.activation(grown[n][:, piece], totals[n][:, piece], FUNC.Exp, bias=bias[:, 0:1])
+
+        def relu(n):
+            kept[n] = work.tile([M, PIECE], F32, name="kept")
+            for piece in WHOLE if n < JOINED_BY_GPSIMD else HALVES:
                 if n < BLOCKS - 1:
-                    nc.scalar.activation(kept[:, piece], total[:, piece], FUNC.Relu, bias=bias[:, 0:1])
+                    nc.scalar.activation(kept[n][:, piece], totals[n][:, piece], FUNC.Relu, bias=bias[:, 0:1])
                 else:
                     nc.vector.tensor_scalar(
-                        kept[:, piece], total[:, piece], bias[:, 0:1], 0.0, op0=ALU.add, op1=ALU.max
+                        kept[n][:, piece], totals[n][:, piece], bias[:, 0:1], 0.0, op0=ALU.add, op1=ALU.max
                     )
-            return grown, kept
 
-        def join(n, grown, kept):
+        def join(n):
             result = work.tile([M, PIECE], F32, name="result")
             if n < JOINED_BY_GPSIMD:
                 lost = work.tile([M, PIECE], F32, name="lost", bufs=JOINED_BY_GPSIMD)
-                nc.scalar.activation(lost[:], grown[:], FUNC.Relu, bias=1.0, scale=-1.0)
-                nc.gpsimd.tensor_sub(result[:], kept[:], lost[:])
+                nc.scalar.activation(lost[:], grown[n][:], FUNC.Relu, bias=1.0, scale=-1.0)
+                nc.gpsimd.tensor_sub(result[:], kept[n][:], lost[:])
                 nc.sync.dma_start(out[:, n * PIECE : (n + 1) * PIECE], result[:])
             else:
                 for half in HALVES:
                     nc.vector.scalar_tensor_tensor(
-                        result[:, half], grown[:, half], -1.0, kept[:, half], op0=ALU.add, op1=ALU.min
+                        result[:, half], grown[n][:, half], -1.0, kept[n][:, half], op0=ALU.add, op1=ALU.min
                     )
                     nc.sync.dma_start(out[:, n * PIECE + half.start : n * PIECE + half.stop], result[:, half])
 
-        totals, parts = {}, {}
-        for step in range(BLOCKS + 2):
-            if step < BLOCKS:
-                totals[step] = add_centre(step, maximum(step))
-            if 0 <= step - 1 < BLOCKS:
-                parts[step - 1] = exp_and_relu(step - 1, totals[step - 1])
-            if 0 <= step - 2:
-                join(step - 2, *parts[step - 2])
+        totals, grown, kept = {}, {}, {}
+        totals[0] = add_centre(0, maximum(0))
+        totals[1] = add_centre(1, maximum(1))
+        exp(0)
+        relu(0)
+        totals[2] = add_centre(2, maximum(2))
+        exp(1)
+        join(0)
+        totals[3] = add_centre(3, maximum(3))
+        relu(1)
+        exp(2)
+        relu(2)
+        join(1)
+        exp(3)
+        relu(3)
+        join(2)
+        join(3)

import concourse.mybir as mybir

BF16, F32, U16 = mybir.dt.bfloat16, mybir.dt.float32, mybir.dt.uint16
ALU = mybir.AluOpType
FUNC = mybir.ActivationFunctionType

C = 128
M = 128
S = 2048
K = 4
N = K * S
PIECE = 512
BLOCKS = S // PIECE
WHOLE = (slice(0, PIECE),)
HALVES = (slice(0, PIECE // 2), slice(PIECE // 2, PIECE))
WARM_UP = 3
JOINED_BY_GPSIMD = BLOCKS // 2
ADDED_BY_GPSIMD = BLOCKS - 2

FLOPS = 2 * C * M * N + 2 * (2 * C * M * S)


def tile_edgeconv_kernel(tc, x, w, w_self, b, offs, out):
    nc = tc.nc
    with (
        tc.tile_pool(name="held", bufs=1) as held,
        tc.tile_pool(name="work", bufs=BLOCKS) as work,
        tc.psum_pool(name="banks", bufs=8) as banks,
    ):
        offsets = held.tile([128, N // 16], U16, name="offsets")
        table = held.tile([C, S], BF16, name="table")
        w_self_sb = held.tile([C, M], BF16, name="w_self_sb")
        w_sb = held.tile([C, M], BF16, name="w_sb")
        bias = held.tile([M, 1], F32, name="bias")
        nc.scalar.dma_start(w_self_sb[:], w_self)
        nc.scalar.dma_start(w_sb[:], w)
        nc.scalar.dma_start(bias[:], b)
        for n in (0, 1):
            nc.sync.dma_start(table[:, n * PIECE : (n + 1) * PIECE], x[:, n * PIECE : (n + 1) * PIECE])
        nc.sync.dma_start(offsets[:], offs)
        nc.sync.dma_start(table[:, 2 * PIECE :], x[:, 2 * PIECE :])

        zeros = held.tile([C, PIECE], BF16, name="zeros")
        nc.vector.memset(zeros[:], 0.0)
        unused = banks.tile([M, PIECE], F32, name="unused", tag="bank")
        for i in range(WARM_UP):
            nc.tensor.matmul(unused[:], zeros[:, 0:M], zeros[:], start=True, stop=True)

        neg_w = held.tile([C, M], BF16, name="neg_w")
        nc.vector.tensor_scalar_mul(neg_w[:], w_sb[:], -1.0)

        def centre_term(n):
            cols = slice(n * PIECE, (n + 1) * PIECE)
            centre_bank = banks.tile([M, PIECE], F32, name="centre_bank", tag="bank")
            nc.tensor.matmul(centre_bank[:], w_self_sb[:], table[:, cols], start=True, stop=False)
            nc.tensor.matmul(centre_bank[:], neg_w[:], table[:, cols], start=False, stop=True)
            return centre_bank

        def maximum(n):
            products = []
            for k in range(K):
                first = (k * S + n * PIECE) // 16
                product = banks.tile([M, PIECE], F32, name="product", tag="bank")
                nc.tensor.matmul(
                    product[:],
                    w_sb[:],
                    table[:].indirect(offsets[:, first : first + PIECE // 16]),
                    start=True,
                    stop=True,
                )
                products.append(product)
            best = work.tile([M, PIECE], F32, name="best", bufs=2)
            for half in HALVES:
                nc.scalar.copy(best[:, half], products[0][:, half])
            for k in range(1, K):
                for half in HALVES:
                    nc.vector.tensor_max(best[:, half], best[:, half], products[k][:, half])
            return best

        centre_banks = {n: centre_term(n) for n in range(BLOCKS - 1)}
        centre = held.tile([M, PIECE], F32, name="centre")
        nc.scalar.copy(centre[:], centre_banks[ADDED_BY_GPSIMD][:])

        def add_centre(n, best):
            total = work.tile([M, PIECE], F32, name="total")
            if n == ADDED_BY_GPSIMD:
                for half in HALVES:
                    nc.gpsimd.tensor_add(total[:, half], best[:, half], centre[:, half])
            else:
                centre_bank = centre_banks[n] if n in centre_banks else centre_term(n)
                for half in HALVES:
                    nc.vector.tensor_add(total[:, half], best[:, half], centre_bank[:, half])
            return total

        def exp(n):
            grown[n] = work.tile([M, PIECE], F32, name="grown")
            for piece in WHOLE if n < JOINED_BY_GPSIMD else HALVES:
                nc.scalar.activation(grown[n][:, piece], totals[n][:, piece], FUNC.Exp, bias=bias[:, 0:1])

        def relu(n):
            kept[n] = work.tile([M, PIECE], F32, name="kept")
            for piece in WHOLE if n < JOINED_BY_GPSIMD else HALVES:
                if n < BLOCKS - 1:
                    nc.scalar.activation(kept[n][:, piece], totals[n][:, piece], FUNC.Relu, bias=bias[:, 0:1])
                else:
                    nc.vector.tensor_scalar(
                        kept[n][:, piece], totals[n][:, piece], bias[:, 0:1], 0.0, op0=ALU.add, op1=ALU.max
                    )

        def join(n):
            result = work.tile([M, PIECE], F32, name="result")
            if n < JOINED_BY_GPSIMD:
                lost = work.tile([M, PIECE], F32, name="lost", bufs=JOINED_BY_GPSIMD)
                nc.scalar.activation(lost[:], grown[n][:], FUNC.Relu, bias=1.0, scale=-1.0)
                nc.gpsimd.tensor_sub(result[:], kept[n][:], lost[:])
                nc.sync.dma_start(out[:, n * PIECE : (n + 1) * PIECE], result[:])
            else:
                for half in HALVES:
                    nc.vector.scalar_tensor_tensor(
                        result[:, half], grown[n][:, half], -1.0, kept[n][:, half], op0=ALU.add, op1=ALU.min
                    )
                    nc.sync.dma_start(out[:, n * PIECE + half.start : n * PIECE + half.stop], result[:, half])

        totals, grown, kept = {}, {}, {}
        totals[0] = add_centre(0, maximum(0))
        totals[1] = add_centre(1, maximum(1))
        exp(0)
        relu(0)
        totals[2] = add_centre(2, maximum(2))
        exp(1)
        join(0)
        totals[3] = add_centre(3, maximum(3))
        relu(1)
        exp(2)
        relu(2)
        join(1)
        exp(3)
        relu(3)
        join(2)
        join(3)
